import numpy as np
import ml_dtypes


def mxq(x, axis, fmt="e4m3"):
    dtype, down = {"e4m3": (ml_dtypes.float8_e4m3fn, 7), "e5m2": (ml_dtypes.float8_e5m2, 14)}[fmt]
    v = np.moveaxis(np.asarray(x, np.float32).astype(ml_dtypes.bfloat16).astype(np.float64), axis, -1)
    blocks = v.reshape(v.shape[:-1] + (-1, 32))
    amax = np.abs(blocks).max(-1, keepdims=True)
    byte = np.maximum(np.where(amax > 0, np.frexp(amax)[1] - 1 + 127, 0) - down, 1)
    scale = np.exp2(byte - 127.0)
    codes = (blocks / scale).astype(np.float32).astype(dtype).astype(np.float64)
    return np.moveaxis((codes * scale).reshape(v.shape), -1, axis)


WIDE = False


def mx_kscale(k):
    if not WIDE:
        return np.ones(k)
    levels = np.array([10, -10, 5, -5, 0])
    a = np.random.permutation(np.resize(levels, k // 512 * 4)).reshape(k // 512, 4)
    idx = np.arange(k)
    return np.exp2(a[idx // 512, idx % 128 // 32])


BF16 = ml_dtypes.bfloat16


def bf(x):
    return np.asarray(x, np.float32).astype(BF16)


def f64(x):
    return np.asarray(x).astype(np.float64)


E2M1 = np.array([0.0, 0.5, 1.0, 1.5, 2.0, 3.0, 4.0, 6.0, -0.0, -0.5, -1.0, -1.5, -2.0, -3.0, -4.0, -6.0])


def pack_weight(w, fmt):
    k, n = w.shape
    w = f64(bf(w)).reshape(k // 32, 32, n)
    amax = np.abs(w).max(1)
    if fmt == "e4m3":
        byte = np.frexp(amax)[1] - 1 + 127 - 7
    else:
        mant, ex = np.frexp(amax / 6.0)
        byte = np.where(mant > 0.5, ex, ex - 1) + 127
    byte = np.clip(np.where(amax > 0, byte, 1), 1, 254)
    scaled = (w * np.exp2(127.0 - byte)[:, None, :]).reshape(k, n).astype(np.float32)
    by_word = np.ascontiguousarray(scaled.reshape(k // 512, 128, 4, n).transpose(0, 1, 3, 2))
    if fmt == "e4m3":
        words = by_word.astype(ml_dtypes.float8_e4m3fn).view(np.uint8)
    else:
        c = by_word.astype(ml_dtypes.float4_e2m1fn).view(np.uint8) & 0xF
        words = c[..., 0::2] | (c[..., 1::2] << 4)
    return np.ascontiguousarray(words), np.ascontiguousarray(byte.astype(np.uint8).reshape(k // 512, 16, n))


def unpack_weight(words, scales, fmt):
    g, p, n, _ = words.shape
    if fmt == "e4m3":
        vals = np.ascontiguousarray(words).view(ml_dtypes.float8_e4m3fn).astype(np.float64)
    else:
        nib = np.empty((g, p, n, 4), np.uint8)
        nib[..., 0::2] = words & 0xF
        nib[..., 1::2] = words >> 4
        vals = E2M1[nib]
    vals = vals * np.repeat(np.exp2(scales.astype(np.float64) - 127.0), 8, axis=1)[..., None]
    return vals.transpose(0, 1, 3, 2).reshape(g * 512, n)


B, T, N, M, A, C, Q, D = 1, 1, 128, 128, 3072, 1024, 4096, 2048
G = A + C
DILATION = 1.5
MIN_EXTENT = 0.5
GATE_TEMP = 3.0
FEAT_TEMP = 6.0
KEEP_W = 0.5
FMT = "e4m3"


def l2norm(x, eps=1e-12):
    n = np.sqrt((x * x).sum(axis=-1, keepdims=True))
    return x / np.maximum(n, eps)


def setup_inputs():
    s, u = mx_kscale(G), mx_kscale(Q)
    d = {}
    d["center"] = bf(np.random.standard_normal((B, T, N * 3)) * 5.0)
    d["instance_affinity"] = bf(np.random.standard_normal((B, T, N, A)) * s[:A])
    d["motion_code"] = bf(np.random.standard_normal((B, T, N, C)) * s[A:])
    d["keep_score"] = bf(np.maximum(np.random.uniform(-0.05, 0.99, (B, T, N)), 0.0))
    d["query_box3d"] = bf(np.random.standard_normal((B, T, M, 7)) * 3.0)
    d["query_feat"] = bf(np.random.standard_normal((B, T, M, Q)) * u)
    d["presence_logit"] = bf(np.random.standard_normal((B, T, M)))
    wq = np.random.standard_normal((D, Q)) / np.sqrt(Q) / u
    d["Wq_words"], d["Wq_scales"] = pack_weight(np.ascontiguousarray(wq.T), FMT)
    d["bq"] = bf(np.random.standard_normal(D) * 0.5)
    wg = np.random.standard_normal((D, G)) / np.sqrt(G) / s
    d["Wg_words"], d["Wg_scales"] = pack_weight(np.ascontiguousarray(wg.T), FMT)
    d["bg"] = bf(np.random.standard_normal(D) * 0.5)
    d["background_bias"] = bf(0.5 + 0.1 * np.random.standard_normal(1))
    return d


def reference(center, instance_affinity, motion_code, keep_score, query_box3d,
              query_feat, presence_logit, Wq_words, Wq_scales, bq, Wg_words, Wg_scales, bg, background_bias):
    b, t = center.shape[:2]
    centers = f64(center).reshape(b, t, -1, 3)
    qbox = f64(query_box3d)[..., :7]
    q_centers = qbox[..., :3]
    q_sizes = np.maximum(np.abs(qbox[..., 3:6]), MIN_EXTENT)

    delta = np.abs(centers[:, :, :, None, :] - q_centers[:, :, None, :, :])
    normalized = delta / (0.5 * DILATION * q_sizes[:, :, None, :, :])
    signed_distance = normalized.max(axis=-1) - 1.0
    gate_logit = np.clip(-signed_distance * GATE_TEMP, -8.0, 8.0)

    gfeat = np.concatenate([f64(instance_affinity), f64(motion_code)], axis=-1)
    gfeat = gfeat.reshape(b, t, -1, gfeat.shape[-1])
    qf = l2norm((mxq(f64(query_feat), 3, "e4m3") @ unpack_weight(Wq_words, Wq_scales, FMT)) + f64(bq))
    gf = l2norm((mxq(gfeat, 3, "e4m3") @ unpack_weight(Wg_words, Wg_scales, FMT)) + f64(bg))
    feature_similarity = mxq(gf, 3, "e4m3") @ mxq(qf, 3, "e4m3").transpose(0, 1, 3, 2)

    presence = f64(presence_logit)[:, :, None, :]
    ks = np.clip(f64(keep_score).reshape(b, t, -1, 1), 1e-4, 1.0 - 1e-4)
    routing_keep = np.log(ks) - np.log1p(-ks)

    fg_logits = presence + FEAT_TEMP * feature_similarity + gate_logit + KEEP_W * routing_keep
    bg_logits = np.zeros_like(fg_logits[..., :1]) + f64(background_bias)
    logits = np.concatenate([bg_logits, fg_logits], axis=-1)
    e = np.exp(logits - logits.max(axis=-1, keepdims=True))
    probs = e / e.sum(axis=-1, keepdims=True)
    return probs.reshape(b, -1, probs.shape[-1])

@@ -1,0 +1,369 @@
+from contextlib import ExitStack
+
+import concourse.mybir as mybir
+from concourse.masks import make_identity
+
+F32 = mybir.dt.float32
+BF16 = mybir.dt.bfloat16
+I32 = mybir.dt.int32
+U32 = mybir.dt.uint32
+U8 = mybir.dt.uint8
+FP8X4 = mybir.dt.float8_e4m3fn_x4
+ALU = mybir.AluOpType
+ACT = mybir.ActivationFunctionType
+AX = mybir.AxisListType
+
+P = 128
+K_IN = 4096
+D_OUT = 2048
+BANK = 512
+PASSES = K_IN // 512
+FLOPS = 2 * (2 * P * K_IN * D_OUT) + 2 * P * P * D_OUT
+
+W_BUFS = 8
+SPLIT = 1536
+SCALES_ON_GPSIMD = False
+
+COL_BQ = 0
+COL_BG = 2048
+COL_BOX = 4096
+COL_PRES = 4992
+COL_CEN = 5120
+COL_KEEP = 5504
+COL_BGB = 5632
+ROW_W = 5664
+
+
+def tile_gaussianqueryassignment_w_kernel(
+    tc,
+    center,
+    instance_affinity,
+    motion_code,
+    keep_score,
+    query_box3d,
+    query_feat,
+    presence_logit,
+    Wq_words,
+    Wq_scales,
+    bq,
+    Wg_words,
+    Wg_scales,
+    bg,
+    background_bias,
+    out,
+):
+    nc = tc.nc
+    with ExitStack() as ctx:
+        keep = ctx.enter_context(tc.tile_pool(name="keep", bufs=1))
+        wpool = ctx.enter_context(tc.tile_pool(name="wpool", bufs=W_BUFS))
+        work = ctx.enter_context(tc.tile_pool(name="work", bufs=2))
+        psum = ctx.enter_context(tc.psum_pool(name="psum", bufs=1))
+
+        words_in = {"q": Wq_words, "g": Wg_words}
+        scales_in = {"q": Wq_scales, "g": Wg_scales}
+
+        planes = {}
+        for which in ("q", "g"):
+            pl = keep.tile([P, 2, D_OUT], U8, name="planes_" + which, align_bytes=64)
+            nc.vector.memset(pl[:].bitcast(I32), 0)
+            planes[which] = pl
+        row = keep.tile([P, ROW_W], BF16, name="row")
+        nc.vector.memset(row[:], 0.0)
+        ones = keep.tile([P, P], BF16, name="ones")
+        nc.vector.memset(ones[:], 1.0)
+        neg_half = keep.tile([P, 1], F32, name="neg_half")
+        nc.vector.memset(neg_half[:], -0.5)
+        ident_f = keep.tile([P, P], F32, name="ident_f")
+        make_identity(nc, ident_f[:])
+        ident_b = keep.tile([P, P], BF16, name="ident_b")
+        make_identity(nc, ident_b[:])
+
+        x_q = keep.tile([P, K_IN], BF16, name="x_q")
+        nc.sync.dma_start(out=x_q[:], in_=query_feat.rearrange("a b m k -> (a b m) k"))
+
+        for which in ("q", "g"):
+            for h in range(2):
+                for quad in range(4):
+                    dst = planes[which][32 * quad : 32 * quad + 16, h, :]
+                    src = scales_in[which][4 * h : 4 * h + 4, 4 * quad : 4 * quad + 4, :]
+                    if SCALES_ON_GPSIMD:
+                        nc.gpsimd.dma_start(out=dst.bitcast(F32), in_=src.bitcast(F32))
+                    else:
+                        nc.sync.dma_start(out=dst.bitcast(I32), in_=src.bitcast(I32))
+
+        x_g = keep.tile([P, K_IN], BF16, name="x_g")
+        nc.sync.dma_start(out=x_g[:, 0:3072], in_=instance_affinity.rearrange("a b n k -> (a b n) k"))
+        nc.sync.dma_start(out=x_g[:, 3072:4096], in_=motion_code.rearrange("a b n k -> (a b n) k"))
+
+        nc.scalar.dma_start(out=row[0:1, COL_BQ : COL_BQ + D_OUT], in_=bq.rearrange("(o n) -> o n", o=1))
+        nc.scalar.dma_start(out=row[0:1, COL_BG : COL_BG + D_OUT], in_=bg.rearrange("(o n) -> o n", o=1))
+        nc.scalar.dma_start(out=row[0:1, COL_BOX : COL_BOX + 896], in_=query_box3d.rearrange("a b m c -> (a b) (m c)"))
+        nc.scalar.dma_start(out=row[0:1, COL_PRES : COL_PRES + P], in_=presence_logit.rearrange("a b m -> (a b) m"))
+        nc.scalar.dma_start(out=row[0:1, COL_CEN : COL_CEN + 384], in_=center.rearrange("a b n -> (a b) n"))
+        nc.scalar.dma_start(out=row[0:1, COL_KEEP : COL_KEEP + P], in_=keep_score.rearrange("a b n -> (a b) n"))
+        nc.scalar.dma_start(out=row[0:1, COL_BGB : COL_BGB + 1], in_=background_bias.rearrange("(o n) -> o n", o=1))
+
+        chunks = (
+            [("q", g, 0, D_OUT) for g in range(PASSES)]
+            + [("g", g, 0, SPLIT) for g in range(PASSES)]
+            + [("g", g, SPLIT, D_OUT) for g in range(PASSES)]
+        )
+        n_big = 2 * PASSES
+        w_tiles = {}
+
+        def load_chunk(i):
+            which, g, n0, n1 = chunks[i]
+            wide = n1 - n0
+            if i < n_big:
+                w = wpool.tile([P, D_OUT], U32, name="w_big", tag="w_big", align_bytes=64)
+            else:
+                w = wpool.tile([P, D_OUT - SPLIT], U32, name="w_small", tag="w_small", align_bytes=64)
+            src = words_in[which][g][:, n0:n1, :].rearrange("p n t -> p (n t)").bitcast(I32)
+            nc.sync.dma_start(out=w[:, 0:wide].bitcast(I32), in_=src)
+            w_tiles[i] = w
+
+        for i in range(W_BUFS):
+            load_chunk(i)
+
+        x_words = {}
+
+        def prep_x(which, x_sb, first_bank):
+            xv = x_sb[:].bitcast(F32)
+            grouped = keep.tile([P, PASSES, P, 4], BF16, name="grouped_" + which, align_bytes=64)
+            xw = keep.tile([P, PASSES * P], U32, name="xw_" + which, align_bytes=64)
+            xs = keep.tile([P, PASSES * P], U8, name="xs_" + which, align_bytes=64)
+            for pair in range(4):
+                xt = psum.tile([P, 2, 2, P], F32, name="xt_" + which, tag="bk%d" % (first_bank + pair))
+                for g2 in range(2):
+                    g = 2 * pair + g2
+                    for u in range(2):
+                        nc.tensor.transpose(xt[:, g2, u, :], xv[:, 256 * g + u : 256 * (g + 1) : 2], ident_f[:])
+                dst = (
+                    grouped[:, 2 * pair : 2 * pair + 2]
+                    .rearrange("p g r t -> p g (r t)")
+                    .bitcast(F32)
+                    .rearrange("p g (r u) -> p g r u", u=2)
+                )
+                src = xt[:].rearrange("p g u r -> p g r u")
+                if pair % 2 == 0:
+                    nc.vector.tensor_copy(out=dst, in_=src)
+                else:
+                    nc.scalar.copy(out=dst, in_=src)
+                    half = pair // 2
+                    nc.vector.quantize_mx(
+                        out=xw[:, 512 * half : 512 * (half + 1)].bitcast(FP8X4),
+                        scales=xs[:, 512 * half : 512 * (half + 1)],
+                        in_=grouped[:, 4 * half : 4 * half + 4].rearrange("p g r t -> p (g r t)"),
+                    )
+            x_words[which] = (xw, xs)
+
+        prep_x("q", x_q, 0)
+        prep_x("g", x_g, 4)
+
+        spread_count = [0]
+
+        def spread(col, n, name):
+            t = psum.tile([P, n], F32, name=name, tag="bk%d" % (4 + spread_count[0] % 4))
+            spread_count[0] = spread_count[0] + 1
+            nc.tensor.matmul(out=t[:], lhsT=ones[:], rhs=row[:, col : col + n], start=True, stop=True)
+            return t
+
+        bias_bc = keep.tile([P, 2 * D_OUT], BF16, name="bias_bc")
+        bias_col = {"q": COL_BQ, "g": COL_BG}
+
+        def spread_bias(which):
+            for b in range(4):
+                col = bias_col[which] + BANK * b
+                t = spread(col, BANK, "bias_ps")
+                if b % 2 == 0:
+                    nc.scalar.copy(out=bias_bc[:, col : col + BANK], in_=t[:])
+                else:
+                    nc.vector.tensor_copy(out=bias_bc[:, col : col + BANK], in_=t[:])
+
+        spread_bias("q")
+
+        boxes = keep.tile([P, 1024], F32, name="boxes")
+        for j in range(2):
+            t = spread(COL_BOX + BANK * j, BANK, "box_ps")
+            nc.scalar.copy(out=boxes[:, BANK * j : BANK * (j + 1)], in_=t[:])
+        box_v = boxes[:, 0:896].rearrange("p (m c) -> p m c", c=7)
+        pres_bc = boxes[:, 896:1024]
+
+        cen_ps = spread(COL_CEN, BANK, "cen_ps")
+        masked = work.tile([P, P, 3], F32, name="masked")
+        nc.vector.tensor_tensor(
+            out=masked[:],
+            in0=cen_ps[:, 0:384].rearrange("p (n c) -> p n c", c=3),
+            in1=ident_f[:].unsqueeze(2).to_broadcast([P, P, 3]),
+            op=ALU.mult,
+        )
+        cen = keep.tile([P, 3], F32, name="cen")
+        nc.vector.tensor_reduce(out=cen[:], in_=masked[:].rearrange("p n c -> p c n"), axis=AX.X, op=ALU.add)
+        masked_k = work.tile([P, P], F32, name="masked_k")
+        nc.vector.tensor_tensor(out=masked_k[:], in0=cen_ps[:, 384:512], in1=ident_f[:], op=ALU.mult)
+        ks = keep.tile([P, 1], F32, name="ks")
+        nc.vector.tensor_reduce(out=ks[:], in_=masked_k[:], axis=AX.X, op=ALU.add)
+
+        logits = keep.tile([P, P + 1], F32, name="logits")
+        bgb_ps = spread(COL_BGB, 32, "bgb_ps")
+        nc.vector.tensor_copy(out=logits[:, 0:1], in_=bgb_ps[:, 0:1])
+
+        spread_bias("g")
+
+        kc = keep.tile([P, 1], F32, name="kc")
+        nc.vector.tensor_scalar(out=kc[:], in0=ks[:], scalar1=1e-4, scalar2=1.0 - 1e-4, op0=ALU.max, op1=ALU.min)
+        ln_k = keep.tile([P, 1], F32, name="ln_k")
+        nc.scalar.activation(out=ln_k[:], in_=kc[:], func=ACT.Ln)
+        ln_1k = keep.tile([P, 1], F32, name="ln_1k")
+        nc.scalar.activation(out=ln_1k[:], in_=kc[:], func=ACT.Ln, bias=1.0, scale=-1.0)
+        warm = keep.tile([P, 1], F32, name="warm")
+        nc.scalar.activation(out=warm[:], in_=ln_1k[:], func=ACT.Exp)
+        half_keep = keep.tile([P, 1], F32, name="half_keep")
+        nc.vector.tensor_scalar(
+            out=half_keep[:], in0=ln_k[:], scalar1=ln_1k[:, 0:1], scalar2=0.5, op0=ALU.subtract, op1=ALU.mult
+        )
+
+        size_v = box_v[:, :, 3:6].rearrange("p m c -> p c m")
+        ext = keep.tile([P, 3, P], F32, name="ext")
+        nc.vector.scalar_tensor_tensor(out=ext[:], in0=size_v, scalar=-1.0, in1=size_v, op0=ALU.mult, op1=ALU.max)
+        nc.vector.tensor_scalar(out=ext[:], in0=ext[:], scalar1=0.5, scalar2=0.75, op0=ALU.max, op1=ALU.mult)
+        inv = keep.tile([P, 3, P], F32, name="inv")
+        nc.vector.reciprocal(out=inv[:], in_=ext[:])
+        dist = keep.tile([P, 3, P], F32, name="dist")
+        for c in range(3):
+            nc.vector.scalar_tensor_tensor(
+                out=dist[:, c, :],
+                in0=box_v[:, :, c],
+                scalar=cen[:, c : c + 1],
+                in1=inv[:, c, :],
+                op0=ALU.subtract,
+                op1=ALU.mult,
+            )
+        adist = keep.tile([P, 3, P], F32, name="adist")
+        nc.vector.scalar_tensor_tensor(out=adist[:], in0=dist[:], scalar=-1.0, in1=dist[:], op0=ALU.mult, op1=ALU.max)
+        far = keep.tile([P, P], F32, name="far")
+        nc.vector.tensor_reduce(out=far[:], in_=adist[:].rearrange("p c m -> p m c"), axis=AX.X, op=ALU.max)
+        gate = keep.tile([P, P], F32, name="gate")
+        nc.vector.tensor_scalar(out=gate[:], in0=far[:], scalar1=-3.0, scalar2=3.0, op0=ALU.mult, op1=ALU.add)
+        nc.vector.tensor_scalar(out=gate[:], in0=gate[:], scalar1=-8.0, scalar2=8.0, op0=ALU.max, op1=ALU.min)
+        base = keep.tile([P, P], F32, name="base")
+        nc.vector.scalar_tensor_tensor(
+            out=base[:], in0=gate[:], scalar=half_keep[:, 0:1], in1=pres_bc, op0=ALU.add, op1=ALU.add
+        )
+
+        acc = {
+            "q": [psum.tile([P, BANK], F32, name="acc_q%d" % b, tag="bk%d" % b) for b in range(4)],
+            "g": [psum.tile([P, BANK], F32, name="acc_g%d" % b, tag="bk%d" % (4 + b)) for b in range(4)],
+        }
+        y = {}
+        ssp = {}
+        for which in ("q", "g"):
+            y[which] = keep.tile([P, D_OUT], F32, name="y_" + which)
+            ssp[which] = keep.tile([P, 4], F32, name="ssp_" + which)
+
+        def passes(i):
+            which, g, n0, n1 = chunks[i]
+            xw, xs = x_words[which]
+            h = g // 4
+            k = 4 * (g % 4)
+            w = w_tiles[i]
+            for b in range(n0 // BANK, n1 // BANK):
+                c0 = BANK * b - n0
+                nc.tensor.matmul_mx(
+                    out=acc[which][b][:],
+                    lhsT=xw[:, P * g : P * (g + 1)].bitcast(FP8X4),
+                    lhsT_scale=xs[:, P * g : P * (g + 1)],
+                    rhs=w[:, c0 : c0 + BANK].bitcast(FP8X4),
+                    rhs_scale=planes[which][k:P, h, BANK * b : BANK * (b + 1)],
+                    start=(g == 0),
+                    stop=(g == PASSES - 1),
+                )
+
+        def bias_and_squares(which, b):
+            cols = slice(BANK * b, BANK * (b + 1))
+            bcols = slice(bias_col[which] + BANK * b, bias_col[which] + BANK * (b + 1))
+            nc.vector.tensor_tensor(out=y[which][:, cols], in0=acc[which][b][:], in1=bias_bc[:, bcols], op=ALU.add)
+            junk = work.tile([P, BANK], F32, name="junk")
+            nc.scalar.activation(out=junk[:], in_=y[which][:, cols], func=ACT.Square, accum_out=ssp[which][:, b : b + 1])
+
+        f_words = {}
+
+        def normalise_and_pack(which):
+            early = keep.tile([P, 1], F32, name="early_" + which)
+            nc.vector.tensor_reduce(out=early[:], in_=ssp[which][:, 0:3], axis=AX.X, op=ALU.add)
+            ss = keep.tile([P, 1], F32, name="ss_" + which)
+            nc.vector.tensor_scalar(
+                out=ss[:], in0=ssp[which][:, 3:4], scalar1=early[:, 0:1], scalar2=1e-24, op0=ALU.add, op1=ALU.max
+            )
+            rn = keep.tile([P, 1], F32, name="rn_" + which)
+            nc.gpsimd.tensor_tensor(out=rn[:], in0=ss[:], in1=neg_half[:], op=ALU.pow)
+
+            fw = keep.tile([P, 4 * P], U32, name="fw_" + which, align_bytes=64)
+            fs = keep.tile([P, 4 * P], U8, name="fs_" + which, align_bytes=64)
+            grp = keep.tile([P, 4, P, 4], BF16, name="grp_" + which, align_bytes=64)
+            for c in range(4):
+                yn = work.tile([P, BANK], BF16, name="yn", tag="yn", bufs=4)
+                src = y[which][:, BANK * c : BANK * (c + 1)]
+                if c % 2 == 0:
+                    nc.vector.tensor_scalar(out=yn[:], in0=src, scalar1=rn[:, 0:1], scalar2=None, op0=ALU.mult)
+                else:
+                    nc.scalar.activation(out=yn[:], in_=src, func=ACT.Copy, scale=rn[:, 0:1])
+                pt = psum.tile([P, 4, P], BF16, name="pt_" + which, tag="bk%d" % c)
+                for t in range(4):
+                    nc.tensor.transpose(pt[:, t, :], yn[:, P * t : P * (t + 1)], ident_b[:])
+                if c % 2 == 0:
+                    nc.scalar.copy(out=grp[:, c], in_=pt[:].rearrange("p t r -> p r t"))
+                else:
+                    nc.vector.tensor_copy(out=grp[:, c], in_=pt[:].rearrange("p t r -> p r t"))
+                nc.vector.quantize_mx(
+                    out=fw[:, P * c : P * (c + 1)].bitcast(FP8X4),
+                    scales=fs[:, P * c : P * (c + 1)],
+                    in_=grp[:, c].rearrange("p r t -> p (r t)"),
+                )
+            f_words[which] = (fw, fs)
+
+        for i in range(len(chunks)):
+            passes(i)
+            nxt = i + W_BUFS
+            if nxt < n_big:
+                load_chunk(nxt)
+            if nxt == n_big - 1:
+                for j in range(n_big, len(chunks)):
+                    load_chunk(j)
+            if i == PASSES - 1:
+                for b in range(4):
+                    bias_and_squares("q", b)
+                normalise_and_pack("q")
+            if i == 2 * PASSES - 1:
+                for b in range(SPLIT // BANK):
+                    bias_and_squares("g", b)
+        for b in range(SPLIT // BANK, 4):
+            bias_and_squares("g", b)
+        normalise_and_pack("g")
+
+        sim = psum.tile([P, P], F32, name="sim", tag="bk4")
+        gw, gs = f_words["g"]
+        qw, qs = f_words["q"]
+        for c in range(4):
+            nc.tensor.matmul_mx(
+                out=sim[:],
+                lhsT=gw[:, P * c : P * (c + 1)].bitcast(FP8X4),
+                lhsT_scale=gs[:, P * c : P * (c + 1)],
+                rhs=qw[:, P * c : P * (c + 1)].bitcast(FP8X4),
+                rhs_scale=qs[:, P * c : P * (c + 1)],
+                start=(c == 0),
+                stop=(c == 3),
+            )
+        nc.vector.scalar_tensor_tensor(
+            out=logits[:, 1 : P + 1], in0=sim[:], scalar=6.0, in1=base[:], op0=ALU.mult, op1=ALU.add
+        )
+        neg_max = keep.tile([P, 1], F32, name="neg_max")
+        nc.vector.tensor_reduce(out=neg_max[:], in_=logits[:], axis=AX.X, op=ALU.max, negate=True)
+        expd = keep.tile([P, P + 1], F32, name="expd")
+        total = keep.tile([P, 1], F32, name="total")
+        nc.scalar.activation(out=expd[:], in_=logits[:], func=ACT.Exp, bias=neg_max[:, 0:1], scale=1.0, accum_out=total[:])
+        inv_total = keep.tile([P, 1], F32, name="inv_total")
+        nc.vector.reciprocal(out=inv_total[:], in_=total[:])
+        probs = keep.tile([P, P + 1], F32, name="probs")
+        nc.vector.tensor_scalar(out=probs[:], in0=expd[:], scalar1=inv_total[:, 0:1], scalar2=None, op0=ALU.mult)
+        nc.sync.dma_start(out=out.rearrange("a n j -> (a n) j"), in_=probs[:])

@@ -22,7 +22,7 @@ FLOPS = 2 * (2 * P * K_IN * D_OUT) + 2 * P * P * D_OUT
 
 W_BUFS = 8
 SPLIT = 1536
-SCALES_ON_GPSIMD = False
+SCALES_ON_GPSIMD = True
 
 COL_BQ = 0
 COL_BG = 2048
@@ -68,7 +68,7 @@ def tile_gaussianqueryassignment_w_kernel(
             nc.vector.memset(pl[:].bitcast(I32), 0)
             planes[which] = pl
         row = keep.tile([P, ROW_W], BF16, name="row")
-        nc.vector.memset(row[:], 0.0)
+        nc.vector.memset(row[:].bitcast(I32), 0)
         ones = keep.tile([P, P], BF16, name="ones")
         nc.vector.memset(ones[:], 1.0)
         neg_half = keep.tile([P, 1], F32, name="neg_half")
@@ -76,7 +76,6 @@ def tile_gaussianqueryassignment_w_kernel(
         ident_f = keep.tile([P, P], F32, name="ident_f")
         make_identity(nc, ident_f[:])
         ident_b = keep.tile([P, P], BF16, name="ident_b")
-        make_identity(nc, ident_b[:])
 
         x_q = keep.tile([P, K_IN], BF16, name="x_q")
         nc.sync.dma_start(out=x_q[:], in_=query_feat.rearrange("a b m k -> (a b m) k"))
@@ -90,18 +89,19 @@ def tile_gaussianqueryassignment_w_kernel(
                         nc.gpsimd.dma_start(out=dst.bitcast(F32), in_=src.bitcast(F32))
                     else:
                         nc.sync.dma_start(out=dst.bitcast(I32), in_=src.bitcast(I32))
+            if which == "q":
+                make_identity(nc, ident_b[:])
 
         x_g = keep.tile([P, K_IN], BF16, name="x_g")
-        nc.sync.dma_start(out=x_g[:, 0:3072], in_=instance_affinity.rearrange("a b n k -> (a b n) k"))
-        nc.sync.dma_start(out=x_g[:, 3072:4096], in_=motion_code.rearrange("a b n k -> (a b n) k"))
-
-        nc.scalar.dma_start(out=row[0:1, COL_BQ : COL_BQ + D_OUT], in_=bq.rearrange("(o n) -> o n", o=1))
-        nc.scalar.dma_start(out=row[0:1, COL_BG : COL_BG + D_OUT], in_=bg.rearrange("(o n) -> o n", o=1))
-        nc.scalar.dma_start(out=row[0:1, COL_BOX : COL_BOX + 896], in_=query_box3d.rearrange("a b m c -> (a b) (m c)"))
-        nc.scalar.dma_start(out=row[0:1, COL_PRES : COL_PRES + P], in_=presence_logit.rearrange("a b m -> (a b) m"))
-        nc.scalar.dma_start(out=row[0:1, COL_CEN : COL_CEN + 384], in_=center.rearrange("a b n -> (a b) n"))
-        nc.scalar.dma_start(out=row[0:1, COL_KEEP : COL_KEEP + P], in_=keep_score.rearrange("a b n -> (a b) n"))
-        nc.scalar.dma_start(out=row[0:1, COL_BGB : COL_BGB + 1], in_=background_bias.rearrange("(o n) -> o n", o=1))
+        row_loads = [
+            (COL_BQ, D_OUT, bq.rearrange("(o n) -> o n", o=1)),
+            (COL_BOX, 896, query_box3d.rearrange("a b m c -> (a b) (m c)")),
+            (COL_PRES, P, presence_logit.rearrange("a b m -> (a b) m")),
+            (COL_CEN, 384, center.rearrange("a b n -> (a b) n")),
+            (COL_KEEP, P, keep_score.rearrange("a b n -> (a b) n")),
+            (COL_BGB, 1, background_bias.rearrange("(o n) -> o n", o=1)),
+            (COL_BG, D_OUT, bg.rearrange("(o n) -> o n", o=1)),
+        ]
 
         chunks = (
             [("q", g, 0, D_OUT) for g in range(PASSES)]
@@ -124,6 +124,12 @@ def tile_gaussianqueryassignment_w_kernel(
 
         for i in range(W_BUFS):
             load_chunk(i)
+            if i == 0:
+                nc.sync.dma_start(out=x_g[:, 0:3072], in_=instance_affinity.rearrange("a b n k -> (a b n) k"))
+                nc.sync.dma_start(out=x_g[:, 3072:4096], in_=motion_code.rearrange("a b n k -> (a b n) k"))
+            else:
+                col, n, vec = row_loads[i - 1]
+                nc.sync.dma_start(out=row[0:1, col : col + n], in_=vec)
 
         x_words = {}
 

@@ -20,18 +20,10 @@ BANK = 512
 PASSES = K_IN // 512
 FLOPS = 2 * (2 * P * K_IN * D_OUT) + 2 * P * P * D_OUT
 
-W_BUFS = 8
-SPLIT = 1536
-SCALES_ON_GPSIMD = True
-
-COL_BQ = 0
-COL_BG = 2048
-COL_BOX = 4096
-COL_PRES = 4992
-COL_CEN = 5120
-COL_KEEP = 5504
-COL_BGB = 5632
-ROW_W = 5664
+ROW_BQ = 0
+ROW_BG = 4
+ROW_BOX = 8
+ROW_PRES = 10
 
 
 def tile_gaussianqueryassignment_w_kernel(
@@ -55,91 +47,102 @@ def tile_gaussianqueryassignment_w_kernel(
     nc = tc.nc
     with ExitStack() as ctx:
         keep = ctx.enter_context(tc.tile_pool(name="keep", bufs=1))
-        wpool = ctx.enter_context(tc.tile_pool(name="wpool", bufs=W_BUFS))
         work = ctx.enter_context(tc.tile_pool(name="work", bufs=2))
         psum = ctx.enter_context(tc.psum_pool(name="psum", bufs=1))
+        ctx.enter_context(tc.manual_schedule())
 
         words_in = {"q": Wq_words, "g": Wg_words}
         scales_in = {"q": Wq_scales, "g": Wg_scales}
 
+        rows = keep.tile([P, BANK], BF16, name="rows")
+        nc.vector.memset(rows[:].bitcast(I32), 0)
         planes = {}
         for which in ("q", "g"):
-            pl = keep.tile([P, 2, D_OUT], U8, name="planes_" + which, align_bytes=64)
-            nc.vector.memset(pl[:].bitcast(I32), 0)
-            planes[which] = pl
-        row = keep.tile([P, ROW_W], BF16, name="row")
-        nc.vector.memset(row[:].bitcast(I32), 0)
-        ones = keep.tile([P, P], BF16, name="ones")
-        nc.vector.memset(ones[:], 1.0)
-        neg_half = keep.tile([P, 1], F32, name="neg_half")
-        nc.vector.memset(neg_half[:], -0.5)
+            planes[which] = keep.tile([P, 2, D_OUT], U8, name="planes_" + which, align_bytes=64)
+            for h in range(2):
+                nc.vector.memset(planes[which][:, h, :].bitcast(I32), 0)
         ident_f = keep.tile([P, P], F32, name="ident_f")
         make_identity(nc, ident_f[:])
         ident_b = keep.tile([P, P], BF16, name="ident_b")
+        nc.vector.tensor_copy(out=ident_b[:], in_=ident_f[:])
+        neg_half = keep.tile([P, 1], F32, name="neg_half")
+        nc.vector.memset(neg_half[:], -0.5)
+        e_sim = keep.tile([P, P + 1], F32, name="e_sim")
+        nc.vector.memset(e_sim[:, 0:1], 1.0)
 
         x_q = keep.tile([P, K_IN], BF16, name="x_q")
+        x_g = keep.tile([P, K_IN], BF16, name="x_g")
         nc.sync.dma_start(out=x_q[:], in_=query_feat.rearrange("a b m k -> (a b m) k"))
+
+        w_tiles = {}
+
+        def load_w(which, g, n0, n1):
+            w = keep.tile([P, n1 - n0], U32, name="w_%s_%d_%d" % (which, g, n0), align_bytes=64)
+            src = words_in[which][g][:, n0:n1, :].rearrange("p n t -> p (n t)").bitcast(I32)
+            nc.sync.dma_start(out=w[:].bitcast(I32), in_=src)
+            w_tiles[(which, g, n0)] = w
+
+        for g in range(PASSES):
+            load_w("q", g, 0, D_OUT)
+            if g == 3:
+                nc.sync.dma_start(out=x_g[:, 0:3072], in_=instance_affinity.rearrange("a b n k -> (a b n) k"))
+                nc.sync.dma_start(out=x_g[:, 3072:4096], in_=motion_code.rearrange("a b n k -> (a b n) k"))
+        for g in range(6):
+            load_w("g", g, 0, D_OUT)
+        last_cols = [(0, 1024), (1024, 1536), (1536, 2048)]
+        for n0, n1 in last_cols:
+            for g in (6, 7):
+                load_w("g", g, n0, n1)
+
+        nc.scalar.dma_start(out=rows[ROW_BQ : ROW_BQ + 4, :], in_=bq.rearrange("(r n) -> r n", r=4))
+        nc.scalar.dma_start(
+            out=rows[ROW_BOX : ROW_BOX + 2, 0:448], in_=query_box3d.rearrange("a b (r m) c -> (a b r) (m c)", r=2)
+        )
+        nc.scalar.dma_start(out=rows[ROW_PRES : ROW_PRES + 1, 0:P], in_=presence_logit.rearrange("a b m -> (a b) m"))
+        nc.scalar.dma_start(out=rows[ROW_BG : ROW_BG + 4, :], in_=bg.rearrange("(r n) -> r n", r=4))
+        cen_b = keep.tile([P, 3], BF16, name="cen_b")
+        nc.scalar.dma_start(out=cen_b[:], in_=center.rearrange("a b (n c) -> (a b n) c", c=3))
+        ks_b = keep.tile([P, 1], BF16, name="ks_b")
+        nc.scalar.dma_start(out=ks_b[:], in_=keep_score.rearrange("a b (n o) -> (a b n) o", o=1))
+        bgb_b = keep.tile([P, 1], BF16, name="bgb_b")
+        nc.scalar.dma_start(out=bgb_b[:], in_=background_bias.partition_broadcast(P))
 
         for which in ("q", "g"):
             for h in range(2):
                 for quad in range(4):
                     dst = planes[which][32 * quad : 32 * quad + 16, h, :]
                     src = scales_in[which][4 * h : 4 * h + 4, 4 * quad : 4 * quad + 4, :]
-                    if SCALES_ON_GPSIMD:
-                        nc.gpsimd.dma_start(out=dst.bitcast(F32), in_=src.bitcast(F32))
-                    else:
-                        nc.sync.dma_start(out=dst.bitcast(I32), in_=src.bitcast(I32))
-            if which == "q":
-                make_identity(nc, ident_b[:])
+                    nc.gpsimd.dma_start(out=dst.bitcast(F32), in_=src.bitcast(F32))
 
-        x_g = keep.tile([P, K_IN], BF16, name="x_g")
-        row_loads = [
-            (COL_BQ, D_OUT, bq.rearrange("(o n) -> o n", o=1)),
-            (COL_BOX, 896, query_box3d.rearrange("a b m c -> (a b) (m c)")),
-            (COL_PRES, P, presence_logit.rearrange("a b m -> (a b) m")),
-            (COL_CEN, 384, center.rearrange("a b n -> (a b) n")),
-            (COL_KEEP, P, keep_score.rearrange("a b n -> (a b) n")),
-            (COL_BGB, 1, background_bias.rearrange("(o n) -> o n", o=1)),
-            (COL_BG, D_OUT, bg.rearrange("(o n) -> o n", o=1)),
-        ]
+        def spread(row, n, bank, name):
+            t = psum.tile([P, n], F32, name=name, tag="bk%d" % bank)
+            nc.tensor.matmul(
+                out=t[:], lhsT=ident_b[:, row : row + 1].to_broadcast([P, P]), rhs=rows[:, 0:n], start=True, stop=True
+            )
+            return t
 
-        chunks = (
-            [("q", g, 0, D_OUT) for g in range(PASSES)]
-            + [("g", g, 0, SPLIT) for g in range(PASSES)]
-            + [("g", g, SPLIT, D_OUT) for g in range(PASSES)]
-        )
-        n_big = 2 * PASSES
-        w_tiles = {}
+        bias_bc = {}
 
-        def load_chunk(i):
-            which, g, n0, n1 = chunks[i]
-            wide = n1 - n0
-            if i < n_big:
-                w = wpool.tile([P, D_OUT], U32, name="w_big", tag="w_big", align_bytes=64)
-            else:
-                w = wpool.tile([P, D_OUT - SPLIT], U32, name="w_small", tag="w_small", align_bytes=64)
-            src = words_in[which][g][:, n0:n1, :].rearrange("p n t -> p (n t)").bitcast(I32)
-            nc.sync.dma_start(out=w[:, 0:wide].bitcast(I32), in_=src)
-            w_tiles[i] = w
-
-        for i in range(W_BUFS):
-            load_chunk(i)
-            if i == 0:
-                nc.sync.dma_start(out=x_g[:, 0:3072], in_=instance_affinity.rearrange("a b n k -> (a b n) k"))
-                nc.sync.dma_start(out=x_g[:, 3072:4096], in_=motion_code.rearrange("a b n k -> (a b n) k"))
-            else:
-                col, n, vec = row_loads[i - 1]
-                nc.sync.dma_start(out=row[0:1, col : col + n], in_=vec)
+        def spread_bias(which, row0):
+            bias_bc[which] = keep.tile([P, D_OUT], BF16, name="bias_bc_" + which)
+            for b in range(4):
+                t = spread(row0 + b, BANK, 4 + b, "bias_ps")
+                dst = bias_bc[which][:, BANK * b : BANK * (b + 1)]
+                if b % 2 == 0:
+                    nc.scalar.copy(out=dst, in_=t[:])
+                else:
+                    nc.vector.tensor_copy(out=dst, in_=t[:])
 
         x_words = {}
 
         def prep_x(which, x_sb, first_bank):
             xv = x_sb[:].bitcast(F32)
-            grouped = keep.tile([P, PASSES, P, 4], BF16, name="grouped_" + which, align_bytes=64)
+            grouped = keep.tile([P, PASSES, P, 4], BF16, name="grouped", tag="grouped", align_bytes=64)
             xw = keep.tile([P, PASSES * P], U32, name="xw_" + which, align_bytes=64)
             xs = keep.tile([P, PASSES * P], U8, name="xs_" + which, align_bytes=64)
-            for pair in range(4):
-                xt = psum.tile([P, 2, 2, P], F32, name="xt_" + which, tag="bk%d" % (first_bank + pair))
+
+            def move(pair):
+                xt = psum.tile([P, 2, 2, P], F32, name="xt", tag="bk%d" % (first_bank + pair))
                 for g2 in range(2):
                     g = 2 * pair + g2
                     for u in range(2):
@@ -152,83 +155,144 @@ def tile_gaussianqueryassignment_w_kernel(
                 )
                 src = xt[:].rearrange("p g u r -> p g r u")
                 if pair % 2 == 0:
-                    nc.vector.tensor_copy(out=dst, in_=src)
-                else:
                     nc.scalar.copy(out=dst, in_=src)
-                    half = pair // 2
-                    nc.vector.quantize_mx(
-                        out=xw[:, 512 * half : 512 * (half + 1)].bitcast(FP8X4),
-                        scales=xs[:, 512 * half : 512 * (half + 1)],
-                        in_=grouped[:, 4 * half : 4 * half + 4].rearrange("p g r t -> p (g r t)"),
-                    )
+                else:
+                    nc.vector.tensor_copy(out=dst, in_=src)
+
+            def quantise(pair):
+                nc.vector.quantize_mx(
+                    out=xw[:, 256 * pair : 256 * (pair + 1)].bitcast(FP8X4),
+                    scales=xs[:, 256 * pair : 256 * (pair + 1)],
+                    in_=grouped[:, 2 * pair : 2 * pair + 2].rearrange("p g r t -> p (g r t)"),
+                )
+
+            move(0)
+            move(1)
+            quantise(0)
+            move(2)
+            move(3)
+            quantise(1)
+            quantise(2)
+            quantise(3)
             x_words[which] = (xw, xs)
 
-        prep_x("q", x_q, 0)
-        prep_x("g", x_g, 4)
+        col_tiles = {
+            "q": [(0, 512, 0), (512, 1024, 1), (1024, 1536, 2), (1536, 2048, 3)],
+            "g": [(0, 512, 4), (512, 1024, 5), (1024, 1536, 6), (1536, 1792, 7), (1792, 2048, 0)],
+        }
+        acc = {}
+        y = {}
+        ssp = {}
 
-        spread_count = [0]
+        def open_acc(which):
+            acc[which] = [
+                psum.tile([P, n1 - n0], F32, name="acc_%s%d" % (which, i), tag="bk%d" % bank)
+                for i, (n0, n1, bank) in enumerate(col_tiles[which])
+            ]
+            y[which] = keep.tile([P, D_OUT], F32, name="y", tag="y")
+            ssp[which] = keep.tile([P, len(acc[which])], F32, name="ssp_" + which)
 
-        def spread(col, n, name):
-            t = psum.tile([P, n], F32, name=name, tag="bk%d" % (4 + spread_count[0] % 4))
-            spread_count[0] = spread_count[0] + 1
-            nc.tensor.matmul(out=t[:], lhsT=ones[:], rhs=row[:, col : col + n], start=True, stop=True)
-            return t
+        def passes(which, g, w0, w1):
+            xw, xs = x_words[which]
+            h = g // 4
+            k = 4 * (g % 4)
+            w = w_tiles[(which, g, w0)]
+            for i, (n0, n1, bank) in enumerate(col_tiles[which]):
+                if n0 < w0 or n1 > w1:
+                    continue
+                nc.tensor.matmul_mx(
+                    out=acc[which][i][:],
+                    lhsT=xw[:, P * g : P * (g + 1)].bitcast(FP8X4),
+                    lhsT_scale=xs[:, P * g : P * (g + 1)],
+                    rhs=w[:, n0 - w0 : n1 - w0].bitcast(FP8X4),
+                    rhs_scale=planes[which][k:P, h, n0:n1],
+                    start=(g == 0),
+                    stop=(g == PASSES - 1),
+                )
 
-        bias_bc = keep.tile([P, 2 * D_OUT], BF16, name="bias_bc")
-        bias_col = {"q": COL_BQ, "g": COL_BG}
+        def bias_and_squares(which, i):
+            n0, n1, bank = col_tiles[which][i]
+            nc.vector.tensor_tensor(
+                out=y[which][:, n0:n1], in0=acc[which][i][:], in1=bias_bc[which][:, n0:n1], op=ALU.add
+            )
+            junk = work.tile([P, BANK], F32, name="junk")
+            nc.scalar.activation(
+                out=junk[:, 0 : n1 - n0], in_=y[which][:, n0:n1], func=ACT.Square, accum_out=ssp[which][:, i : i + 1]
+            )
 
-        def spread_bias(which):
-            for b in range(4):
-                col = bias_col[which] + BANK * b
-                t = spread(col, BANK, "bias_ps")
-                if b % 2 == 0:
-                    nc.scalar.copy(out=bias_bc[:, col : col + BANK], in_=t[:])
+        f_words = {}
+
+        def inverse_norm(which):
+            last = len(acc[which]) - 1
+            early = keep.tile([P, 1], F32, name="early_" + which)
+            nc.vector.tensor_reduce(out=early[:], in_=ssp[which][:, 0:last], axis=AX.X, op=ALU.add)
+            ss = keep.tile([P, 1], F32, name="ss_" + which)
+            nc.vector.tensor_scalar(
+                out=ss[:],
+                in0=ssp[which][:, last : last + 1],
+                scalar1=early[:, 0:1],
+                scalar2=1e-24,
+                op0=ALU.add,
+                op1=ALU.max,
+            )
+            rn = keep.tile([P, 1], F32, name="rn_" + which)
+            nc.gpsimd.tensor_tensor(out=rn[:], in0=ss[:], in1=neg_half[:], op=ALU.pow)
+            return rn
+
+        def pack(which, rn, banks):
+            fw = keep.tile([P, 4 * P], U32, name="fw_" + which, align_bytes=64)
+            fs = keep.tile([P, 4 * P], U8, name="fs_" + which, align_bytes=64)
+            grp = keep.tile([P, 4, P, 4], BF16, name="grp", tag="grp", align_bytes=64)
+            yn = keep.tile([P, D_OUT], BF16, name="yn", tag="yn")
+            for c in (0, 2, 3, 1):
+                cols = slice(BANK * c, BANK * (c + 1))
+                if c == 1:
+                    nc.scalar.activation(out=yn[:, cols], in_=y[which][:, cols], func=ACT.Copy, scale=rn[:, 0:1])
                 else:
-                    nc.vector.tensor_copy(out=bias_bc[:, col : col + BANK], in_=t[:])
+                    nc.vector.tensor_scalar(
+                        out=yn[:, cols], in0=y[which][:, cols], scalar1=rn[:, 0:1], scalar2=None, op0=ALU.mult
+                    )
+            for c in range(4):
+                pt = psum.tile([P, 4, P], BF16, name="pt_" + which, tag="bk%d" % banks[c])
+                for t in range(4):
+                    nc.tensor.transpose(pt[:, t, :], yn[:, BANK * c + P * t : BANK * c + P * (t + 1)], ident_b[:])
+                if c == 1:
+                    nc.vector.tensor_copy(out=grp[:, c], in_=pt[:].rearrange("p t r -> p r t"))
+                else:
+                    nc.scalar.copy(out=grp[:, c], in_=pt[:].rearrange("p t r -> p r t"))
+            for c in range(4):
+                nc.vector.quantize_mx(
+                    out=fw[:, P * c : P * (c + 1)].bitcast(FP8X4),
+                    scales=fs[:, P * c : P * (c + 1)],
+                    in_=grp[:, c].rearrange("p r t -> p (r t)"),
+                )
+            f_words[which] = (fw, fs)
 
-        spread_bias("q")
+        spread_bias("q", ROW_BQ)
+        prep_x("q", x_q, 0)
 
-        boxes = keep.tile([P, 1024], F32, name="boxes")
+        boxes = keep.tile([P, 2, 448], F32, name="boxes")
         for j in range(2):
-            t = spread(COL_BOX + BANK * j, BANK, "box_ps")
-            nc.scalar.copy(out=boxes[:, BANK * j : BANK * (j + 1)], in_=t[:])
-        box_v = boxes[:, 0:896].rearrange("p (m c) -> p m c", c=7)
-        pres_bc = boxes[:, 896:1024]
+            t = spread(ROW_BOX + j, 448, 4 + j, "box_ps")
+            nc.scalar.copy(out=boxes[:, j, :], in_=t[:])
+        box_v = boxes[:].rearrange("p j (m c) -> p (j m) c", c=7)
+        pres_bc = keep.tile([P, P], F32, name="pres_bc")
+        t = spread(ROW_PRES, P, 6, "pres_ps")
+        nc.scalar.copy(out=pres_bc[:], in_=t[:])
 
-        cen_ps = spread(COL_CEN, BANK, "cen_ps")
-        masked = work.tile([P, P, 3], F32, name="masked")
-        nc.vector.tensor_tensor(
-            out=masked[:],
-            in0=cen_ps[:, 0:384].rearrange("p (n c) -> p n c", c=3),
-            in1=ident_f[:].unsqueeze(2).to_broadcast([P, P, 3]),
-            op=ALU.mult,
-        )
-        cen = keep.tile([P, 3], F32, name="cen")
-        nc.vector.tensor_reduce(out=cen[:], in_=masked[:].rearrange("p n c -> p c n"), axis=AX.X, op=ALU.add)
-        masked_k = work.tile([P, P], F32, name="masked_k")
-        nc.vector.tensor_tensor(out=masked_k[:], in0=cen_ps[:, 384:512], in1=ident_f[:], op=ALU.mult)
-        ks = keep.tile([P, 1], F32, name="ks")
-        nc.vector.tensor_reduce(out=ks[:], in_=masked_k[:], axis=AX.X, op=ALU.add)
-
-        logits = keep.tile([P, P + 1], F32, name="logits")
-        bgb_ps = spread(COL_BGB, 32, "bgb_ps")
-        nc.vector.tensor_copy(out=logits[:, 0:1], in_=bgb_ps[:, 0:1])
-
-        spread_bias("g")
+        open_acc("q")
+        passes("q", 0, 0, D_OUT)
+        spread_bias("g", ROW_BG)
 
         kc = keep.tile([P, 1], F32, name="kc")
-        nc.vector.tensor_scalar(out=kc[:], in0=ks[:], scalar1=1e-4, scalar2=1.0 - 1e-4, op0=ALU.max, op1=ALU.min)
+        nc.vector.tensor_scalar(out=kc[:], in0=ks_b[:], scalar1=1e-4, scalar2=1.0 - 1e-4, op0=ALU.max, op1=ALU.min)
         ln_k = keep.tile([P, 1], F32, name="ln_k")
         nc.scalar.activation(out=ln_k[:], in_=kc[:], func=ACT.Ln)
         ln_1k = keep.tile([P, 1], F32, name="ln_1k")
         nc.scalar.activation(out=ln_1k[:], in_=kc[:], func=ACT.Ln, bias=1.0, scale=-1.0)
-        warm = keep.tile([P, 1], F32, name="warm")
-        nc.scalar.activation(out=warm[:], in_=ln_1k[:], func=ACT.Exp)
-        half_keep = keep.tile([P, 1], F32, name="half_keep")
-        nc.vector.tensor_scalar(
-            out=half_keep[:], in0=ln_k[:], scalar1=ln_1k[:, 0:1], scalar2=0.5, op0=ALU.subtract, op1=ALU.mult
-        )
 
+        cen = keep.tile([P, 3], F32, name="cen")
+        nc.vector.tensor_copy(out=cen[:], in_=cen_b[:])
         size_v = box_v[:, :, 3:6].rearrange("p m c -> p c m")
         ext = keep.tile([P, 3, P], F32, name="ext")
         nc.vector.scalar_tensor_tensor(out=ext[:], in0=size_v, scalar=-1.0, in1=size_v, op0=ALU.mult, op1=ALU.max)
@@ -252,100 +316,43 @@ def tile_gaussianqueryassignment_w_kernel(
         gate = keep.tile([P, P], F32, name="gate")
         nc.vector.tensor_scalar(out=gate[:], in0=far[:], scalar1=-3.0, scalar2=3.0, op0=ALU.mult, op1=ALU.add)
         nc.vector.tensor_scalar(out=gate[:], in0=gate[:], scalar1=-8.0, scalar2=8.0, op0=ALU.max, op1=ALU.min)
-        base = keep.tile([P, P], F32, name="base")
-        nc.vector.scalar_tensor_tensor(
-            out=base[:], in0=gate[:], scalar=half_keep[:, 0:1], in1=pres_bc, op0=ALU.add, op1=ALU.add
+        half_keep = keep.tile([P, 1], F32, name="half_keep")
+        nc.vector.tensor_scalar(
+            out=half_keep[:], in0=ln_k[:], scalar1=ln_1k[:, 0:1], scalar2=0.5, op0=ALU.subtract, op1=ALU.mult
         )
+        base = keep.tile([P, P + 1], F32, name="base")
+        nc.vector.tensor_copy(out=base[:, 0:1], in_=bgb_b[:])
+        nc.vector.scalar_tensor_tensor(
+            out=base[:, 1 : P + 1], in0=gate[:], scalar=half_keep[:, 0:1], in1=pres_bc[:], op0=ALU.add, op1=ALU.add
+        )
+        neg_max = keep.tile([P, 1], F32, name="neg_max")
+        nc.vector.tensor_reduce(out=neg_max[:], in_=base[:], axis=AX.X, op=ALU.max, negate=True)
+        e_base = keep.tile([P, P + 1], F32, name="e_base")
+        nc.scalar.activation(out=e_base[:], in_=base[:], func=ACT.Exp, bias=neg_max[:, 0:1], scale=1.0)
 
-        acc = {
-            "q": [psum.tile([P, BANK], F32, name="acc_q%d" % b, tag="bk%d" % b) for b in range(4)],
-            "g": [psum.tile([P, BANK], F32, name="acc_g%d" % b, tag="bk%d" % (4 + b)) for b in range(4)],
-        }
-        y = {}
-        ssp = {}
-        for which in ("q", "g"):
-            y[which] = keep.tile([P, D_OUT], F32, name="y_" + which)
-            ssp[which] = keep.tile([P, 4], F32, name="ssp_" + which)
+        for g in range(1, 4):
+            passes("q", g, 0, D_OUT)
+        prep_x("g", x_g, 4)
+        for g in range(4, PASSES):
+            passes("q", g, 0, D_OUT)
+        for i in range(4):
+            bias_and_squares("q", i)
+        rn_q = inverse_norm("q")
 
-        def passes(i):
-            which, g, n0, n1 = chunks[i]
-            xw, xs = x_words[which]
-            h = g // 4
-            k = 4 * (g % 4)
-            w = w_tiles[i]
-            for b in range(n0 // BANK, n1 // BANK):
-                c0 = BANK * b - n0
-                nc.tensor.matmul_mx(
-                    out=acc[which][b][:],
-                    lhsT=xw[:, P * g : P * (g + 1)].bitcast(FP8X4),
-                    lhsT_scale=xs[:, P * g : P * (g + 1)],
-                    rhs=w[:, c0 : c0 + BANK].bitcast(FP8X4),
-                    rhs_scale=planes[which][k:P, h, BANK * b : BANK * (b + 1)],
-                    start=(g == 0),
-                    stop=(g == PASSES - 1),
-                )
-
-        def bias_and_squares(which, b):
-            cols = slice(BANK * b, BANK * (b + 1))
-            bcols = slice(bias_col[which] + BANK * b, bias_col[which] + BANK * (b + 1))
-            nc.vector.tensor_tensor(out=y[which][:, cols], in0=acc[which][b][:], in1=bias_bc[:, bcols], op=ALU.add)
-            junk = work.tile([P, BANK], F32, name="junk")
-            nc.scalar.activation(out=junk[:], in_=y[which][:, cols], func=ACT.Square, accum_out=ssp[which][:, b : b + 1])
-
-        f_words = {}
-
-        def normalise_and_pack(which):
-            early = keep.tile([P, 1], F32, name="early_" + which)
-            nc.vector.tensor_reduce(out=early[:], in_=ssp[which][:, 0:3], axis=AX.X, op=ALU.add)
-            ss = keep.tile([P, 1], F32, name="ss_" + which)
-            nc.vector.tensor_scalar(
-                out=ss[:], in0=ssp[which][:, 3:4], scalar1=early[:, 0:1], scalar2=1e-24, op0=ALU.add, op1=ALU.max
-            )
-            rn = keep.tile([P, 1], F32, name="rn_" + which)
-            nc.gpsimd.tensor_tensor(out=rn[:], in0=ss[:], in1=neg_half[:], op=ALU.pow)
-
-            fw = keep.tile([P, 4 * P], U32, name="fw_" + which, align_bytes=64)
-            fs = keep.tile([P, 4 * P], U8, name="fs_" + which, align_bytes=64)
-            grp = keep.tile([P, 4, P, 4], BF16, name="grp_" + which, align_bytes=64)
-            for c in range(4):
-                yn = work.tile([P, BANK], BF16, name="yn", tag="yn", bufs=4)
-                src = y[which][:, BANK * c : BANK * (c + 1)]
-                if c % 2 == 0:
-                    nc.vector.tensor_scalar(out=yn[:], in0=src, scalar1=rn[:, 0:1], scalar2=None, op0=ALU.mult)
-                else:
-                    nc.scalar.activation(out=yn[:], in_=src, func=ACT.Copy, scale=rn[:, 0:1])
-                pt = psum.tile([P, 4, P], BF16, name="pt_" + which, tag="bk%d" % c)
-                for t in range(4):
-                    nc.tensor.transpose(pt[:, t, :], yn[:, P * t : P * (t + 1)], ident_b[:])
-                if c % 2 == 0:
-                    nc.scalar.copy(out=grp[:, c], in_=pt[:].rearrange("p t r -> p r t"))
-                else:
-                    nc.vector.tensor_copy(out=grp[:, c], in_=pt[:].rearrange("p t r -> p r t"))
-                nc.vector.quantize_mx(
-                    out=fw[:, P * c : P * (c + 1)].bitcast(FP8X4),
-                    scales=fs[:, P * c : P * (c + 1)],
-                    in_=grp[:, c].rearrange("p r t -> p (r t)"),
-                )
-            f_words[which] = (fw, fs)
-
-        for i in range(len(chunks)):
-            passes(i)
-            nxt = i + W_BUFS
-            if nxt < n_big:
-                load_chunk(nxt)
-            if nxt == n_big - 1:
-                for j in range(n_big, len(chunks)):
-                    load_chunk(j)
-            if i == PASSES - 1:
-                for b in range(4):
-                    bias_and_squares("q", b)
-                normalise_and_pack("q")
-            if i == 2 * PASSES - 1:
-                for b in range(SPLIT // BANK):
-                    bias_and_squares("g", b)
-        for b in range(SPLIT // BANK, 4):
-            bias_and_squares("g", b)
-        normalise_and_pack("g")
+        open_acc("g")
+        passes("g", 0, 0, D_OUT)
+        passes("g", 1, 0, D_OUT)
+        pack("q", rn_q, [1, 2, 3, 1])
+        for g in range(2, 6):
+            passes("g", g, 0, D_OUT)
+        for n0, n1 in last_cols:
+            for g in (6, 7):
+                passes("g", g, n0, n1)
+            for i, (c0, c1, bank) in enumerate(col_tiles["g"]):
+                if n0 <= c0 and c1 <= n1:
+                    bias_and_squares("g", i)
+        rn_g = inverse_norm("g")
+        pack("g", rn_g, [1, 2, 3, 5])
 
         sim = psum.tile([P, P], F32, name="sim", tag="bk4")
         gw, gs = f_words["g"]
@@ -360,16 +367,14 @@ def tile_gaussianqueryassignment_w_kernel(
                 start=(c == 0),
                 stop=(c == 3),
             )
-        nc.vector.scalar_tensor_tensor(
-            out=logits[:, 1 : P + 1], in0=sim[:], scalar=6.0, in1=base[:], op0=ALU.mult, op1=ALU.add
-        )
-        neg_max = keep.tile([P, 1], F32, name="neg_max")
-        nc.vector.tensor_reduce(out=neg_max[:], in_=logits[:], axis=AX.X, op=ALU.max, negate=True)
-        expd = keep.tile([P, P + 1], F32, name="expd")
+        nc.scalar.activation(out=e_sim[:, 1 : P + 1], in_=sim[:], func=ACT.Exp, scale=6.0)
+        prod = keep.tile([P, P + 1], F32, name="prod")
         total = keep.tile([P, 1], F32, name="total")
-        nc.scalar.activation(out=expd[:], in_=logits[:], func=ACT.Exp, bias=neg_max[:, 0:1], scale=1.0, accum_out=total[:])
+        nc.vector.scalar_tensor_tensor(
+            out=prod[:], in0=e_sim[:], scalar=1.0, in1=e_base[:], op0=ALU.mult, op1=ALU.mult, accum_out=total[:]
+        )
         inv_total = keep.tile([P, 1], F32, name="inv_total")
         nc.vector.reciprocal(out=inv_total[:], in_=total[:])
         probs = keep.tile([P, P + 1], F32, name="probs")
-        nc.vector.tensor_scalar(out=probs[:], in0=expd[:], scalar1=inv_total[:, 0:1], scalar2=None, op0=ALU.mult)
+        nc.vector.tensor_scalar(out=probs[:], in0=prod[:], scalar1=inv_total[:, 0:1], scalar2=None, op0=ALU.mult)
         nc.sync.dma_start(out=out.rearrange("a n j -> (a n) j"), in_=probs[:])

@@ -20,6 +20,8 @@ BANK = 512
 PASSES = K_IN // 512
 FLOPS = 2 * (2 * P * K_IN * D_OUT) + 2 * P * P * D_OUT
 
+WARM = 7
+
 ROW_BQ = 0
 ROW_BG = 4
 ROW_BOX = 8
@@ -352,6 +354,9 @@ def tile_gaussianqueryassignment_w_kernel(
                 if n0 <= c0 and c1 <= n1:
                     bias_and_squares("g", i)
         rn_g = inverse_norm("g")
+        warm = psum.tile([P, BANK], F32, name="warm", tag="bk4")
+        for i in range(WARM):
+            nc.tensor.matmul(out=warm[:], lhsT=ident_b[:], rhs=bias_bc["g"][:, 0:BANK], start=True, stop=True)
         pack("g", rn_g, [1, 2, 3, 5])
 
         sim = psum.tile([P, P], F32, name="sim", tag="bk4")

@@ -20,7 +20,7 @@ BANK = 512
 PASSES = K_IN // 512
 FLOPS = 2 * (2 * P * K_IN * D_OUT) + 2 * P * P * D_OUT
 
-WARM = 7
+WARM = 6
 
 ROW_BQ = 0
 ROW_BG = 4
@@ -228,17 +228,16 @@ def tile_gaussianqueryassignment_w_kernel(
             last = len(acc[which]) - 1
             early = keep.tile([P, 1], F32, name="early_" + which)
             nc.vector.tensor_reduce(out=early[:], in_=ssp[which][:, 0:last], axis=AX.X, op=ALU.add)
-            ss = keep.tile([P, 1], F32, name="ss_" + which)
-            nc.vector.tensor_scalar(
-                out=ss[:],
-                in0=ssp[which][:, last : last + 1],
-                scalar1=early[:, 0:1],
-                scalar2=1e-24,
-                op0=ALU.add,
-                op1=ALU.max,
+            raw = keep.tile([P, 1], F32, name="raw_" + which)
+            nc.scalar.activation(
+                out=raw[:],
+                in_=ssp[which][:, last : last + 1],
+                func=ACT.Abs_reciprocal_sqrt,
+                bias=early[:, 0:1],
+                scale=1.0,
             )
             rn = keep.tile([P, 1], F32, name="rn_" + which)
-            nc.gpsimd.tensor_tensor(out=rn[:], in0=ss[:], in1=neg_half[:], op=ALU.pow)
+            nc.vector.tensor_scalar(out=rn[:], in0=raw[:], scalar1=1e12, scalar2=None, op0=ALU.min)
             return rn
 
         def pack(which, rn, banks):
@@ -246,19 +245,16 @@ def tile_gaussianqueryassignment_w_kernel(
             fs = keep.tile([P, 4 * P], U8, name="fs_" + which, align_bytes=64)
             grp = keep.tile([P, 4, P, 4], BF16, name="grp", tag="grp", align_bytes=64)
             yn = keep.tile([P, D_OUT], BF16, name="yn", tag="yn")
-            for c in (0, 2, 3, 1):
+            for c in range(4):
                 cols = slice(BANK * c, BANK * (c + 1))
-                if c == 1:
-                    nc.scalar.activation(out=yn[:, cols], in_=y[which][:, cols], func=ACT.Copy, scale=rn[:, 0:1])
-                else:
-                    nc.vector.tensor_scalar(
-                        out=yn[:, cols], in0=y[which][:, cols], scalar1=rn[:, 0:1], scalar2=None, op0=ALU.mult
-                    )
+                nc.vector.tensor_scalar(
+                    out=yn[:, cols], in0=y[which][:, cols], scalar1=rn[:, 0:1], scalar2=None, op0=ALU.mult
+                )
             for c in range(4):
                 pt = psum.tile([P, 4, P], BF16, name="pt_" + which, tag="bk%d" % banks[c])
                 for t in range(4):
                     nc.tensor.transpose(pt[:, t, :], yn[:, BANK * c + P * t : BANK * c + P * (t + 1)], ident_b[:])
-                if c == 1:
+                if c < 2:
                     nc.vector.tensor_copy(out=grp[:, c], in_=pt[:].rearrange("p t r -> p r t"))
                 else:
                     nc.scalar.copy(out=grp[:, c], in_=pt[:].rearrange("p t r -> p r t"))
@@ -354,6 +350,8 @@ def tile_gaussianqueryassignment_w_kernel(
                 if n0 <= c0 and c1 <= n1:
                     bias_and_squares("g", i)
         rn_g = inverse_norm("g")
+        table = keep.tile([P, 1], F32, name="table")
+        nc.scalar.activation(out=table[:], in_=neg_half[:], func=ACT.Exp)
         warm = psum.tile([P, BANK], F32, name="warm", tag="bk4")
         for i in range(WARM):
             nc.tensor.matmul(out=warm[:], lhsT=ident_b[:], rhs=bias_bc["g"][:, 0:BANK], start=True, stop=True)

@@ -20,7 +20,7 @@ BANK = 512
 PASSES = K_IN // 512
 FLOPS = 2 * (2 * P * K_IN * D_OUT) + 2 * P * P * D_OUT
 
-WARM = 6
+WARM = 7
 
 ROW_BQ = 0
 ROW_BG = 4
@@ -91,9 +91,14 @@ def tile_gaussianqueryassignment_w_kernel(
                 nc.sync.dma_start(out=x_g[:, 3072:4096], in_=motion_code.rearrange("a b n k -> (a b n) k"))
         for g in range(6):
             load_w("g", g, 0, D_OUT)
-        last_cols = [(0, 1024), (1024, 1536), (1536, 2048)]
-        for n0, n1 in last_cols:
-            for g in (6, 7):
+        last_pieces = [
+            [(6, 0, 1024), (7, 0, 1024)],
+            [(6, 1024, 1536), (7, 1024, 1536)],
+            [(6, 1536, 2048), (7, 1536, 1792)],
+            [(7, 1792, 2048)],
+        ]
+        for pieces in last_pieces:
+            for g, n0, n1 in pieces:
                 load_w("g", g, n0, n1)
 
         nc.scalar.dma_start(out=rows[ROW_BQ : ROW_BQ + 4, :], in_=bq.rearrange("(r n) -> r n", r=4))
@@ -250,14 +255,17 @@ def tile_gaussianqueryassignment_w_kernel(
                 nc.vector.tensor_scalar(
                     out=yn[:, cols], in0=y[which][:, cols], scalar1=rn[:, 0:1], scalar2=None, op0=ALU.mult
                 )
+            yw = yn[:].bitcast(F32)
             for c in range(4):
-                pt = psum.tile([P, 4, P], BF16, name="pt_" + which, tag="bk%d" % banks[c])
-                for t in range(4):
-                    nc.tensor.transpose(pt[:, t, :], yn[:, BANK * c + P * t : BANK * c + P * (t + 1)], ident_b[:])
+                pt = psum.tile([P, 2, P], F32, name="pt_" + which, tag="bk%d" % banks[c])
+                for u in range(2):
+                    nc.tensor.transpose(pt[:, u, :], yw[:, 256 * c + P * u : 256 * c + P * (u + 1)], ident_f[:])
+                dst = grp[:, c].rearrange("p r t -> p (r t)").bitcast(F32).rearrange("p (r u) -> p r u", u=2)
+                src = pt[:].rearrange("p u r -> p r u")
                 if c < 2:
-                    nc.vector.tensor_copy(out=grp[:, c], in_=pt[:].rearrange("p t r -> p r t"))
+                    nc.vector.tensor_copy(out=dst, in_=src)
                 else:
-                    nc.scalar.copy(out=grp[:, c], in_=pt[:].rearrange("p t r -> p r t"))
+                    nc.scalar.copy(out=dst, in_=src)
             for c in range(4):
                 nc.vector.quantize_mx(
                     out=fw[:, P * c : P * (c + 1)].bitcast(FP8X4),
@@ -343,12 +351,15 @@ def tile_gaussianqueryassignment_w_kernel(
         pack("q", rn_q, [1, 2, 3, 1])
         for g in range(2, 6):
             passes("g", g, 0, D_OUT)
-        for n0, n1 in last_cols:
-            for g in (6, 7):
+        done = 0
+        for pieces in last_pieces:
+            for g, n0, n1 in pieces:
                 passes("g", g, n0, n1)
-            for i, (c0, c1, bank) in enumerate(col_tiles["g"]):
-                if n0 <= c0 and c1 <= n1:
-                    bias_and_squares("g", i)
+            while col_tiles["g"][done][1] < n1:
+                bias_and_squares("g", done)
+                done += 1
+            bias_and_squares("g", done)
+            done += 1
         rn_g = inverse_norm("g")
         table = keep.tile([P, 1], F32, name="table")
         nc.scalar.activation(out=table[:], in_=neg_half[:], func=ACT.Exp)

from contextlib import ExitStack

import concourse.mybir as mybir
from concourse.masks import make_identity

F32 = mybir.dt.float32
BF16 = mybir.dt.bfloat16
I32 = mybir.dt.int32
U32 = mybir.dt.uint32
U8 = mybir.dt.uint8
FP8X4 = mybir.dt.float8_e4m3fn_x4
ALU = mybir.AluOpType
ACT = mybir.ActivationFunctionType
AX = mybir.AxisListType

P = 128
K_IN = 4096
D_OUT = 2048
BANK = 512
PASSES = K_IN // 512
FLOPS = 2 * (2 * P * K_IN * D_OUT) + 2 * P * P * D_OUT

WARM = 7

ROW_BQ = 0
ROW_BG = 4
ROW_BOX = 8
ROW_PRES = 10


def tile_gaussianqueryassignment_w_kernel(
    tc,
    center,
    instance_affinity,
    motion_code,
    keep_score,
    query_box3d,
    query_feat,
    presence_logit,
    Wq_words,
    Wq_scales,
    bq,
    Wg_words,
    Wg_scales,
    bg,
    background_bias,
    out,
):
    nc = tc.nc
    with ExitStack() as ctx:
        keep = ctx.enter_context(tc.tile_pool(name="keep", bufs=1))
        work = ctx.enter_context(tc.tile_pool(name="work", bufs=2))
        psum = ctx.enter_context(tc.psum_pool(name="psum", bufs=1))
        ctx.enter_context(tc.manual_schedule())

        words_in = {"q": Wq_words, "g": Wg_words}
        scales_in = {"q": Wq_scales, "g": Wg_scales}

        rows = keep.tile([P, BANK], BF16, name="rows")
        nc.vector.memset(rows[:].bitcast(I32), 0)
        planes = {}
        for which in ("q", "g"):
            planes[which] = keep.tile([P, 2, D_OUT], U8, name="planes_" + which, align_bytes=64)
            for h in range(2):
                nc.vector.memset(planes[which][:, h, :].bitcast(I32), 0)
        ident_f = keep.tile([P, P], F32, name="ident_f")
        make_identity(nc, ident_f[:])
        ident_b = keep.tile([P, P], BF16, name="ident_b")
        nc.vector.tensor_copy(out=ident_b[:], in_=ident_f[:])
        neg_half = keep.tile([P, 1], F32, name="neg_half")
        nc.vector.memset(neg_half[:], -0.5)
        e_sim = keep.tile([P, P + 1], F32, name="e_sim")
        nc.vector.memset(e_sim[:, 0:1], 1.0)

        x_q = keep.tile([P, K_IN], BF16, name="x_q")
        x_g = keep.tile([P, K_IN], BF16, name="x_g")
        nc.sync.dma_start(out=x_q[:], in_=query_feat.rearrange("a b m k -> (a b m) k"))

        w_tiles = {}

        def load_w(which, g, n0, n1):
            w = keep.tile([P, n1 - n0], U32, name="w_%s_%d_%d" % (which, g, n0), align_bytes=64)
            src = words_in[which][g][:, n0:n1, :].rearrange("p n t -> p (n t)").bitcast(I32)
            nc.sync.dma_start(out=w[:].bitcast(I32), in_=src)
            w_tiles[(which, g, n0)] = w

        for g in range(PASSES):
            load_w("q", g, 0, D_OUT)
            if g == 3:
                nc.sync.dma_start(out=x_g[:, 0:3072], in_=instance_affinity.rearrange("a b n k -> (a b n) k"))
                nc.sync.dma_start(out=x_g[:, 3072:4096], in_=motion_code.rearrange("a b n k -> (a b n) k"))
        for g in range(6):
            load_w("g", g, 0, D_OUT)
        last_pieces = [
            [(6, 0, 1024), (7, 0, 1024)],
            [(6, 1024, 1536), (7, 1024, 1536)],
            [(6, 1536, 2048), (7, 1536, 1792)],
            [(7, 1792, 2048)],
        ]
        for pieces in last_pieces:
            for g, n0, n1 in pieces:
                load_w("g", g, n0, n1)

        nc.scalar.dma_start(out=rows[ROW_BQ : ROW_BQ + 4, :], in_=bq.rearrange("(r n) -> r n", r=4))
        nc.scalar.dma_start(
            out=rows[ROW_BOX : ROW_BOX + 2, 0:448], in_=query_box3d.rearrange("a b (r m) c -> (a b r) (m c)", r=2)
        )
        nc.scalar.dma_start(out=rows[ROW_PRES : ROW_PRES + 1, 0:P], in_=presence_logit.rearrange("a b m -> (a b) m"))
        nc.scalar.dma_start(out=rows[ROW_BG : ROW_BG + 4, :], in_=bg.rearrange("(r n) -> r n", r=4))
        cen_b = keep.tile([P, 3], BF16, name="cen_b")
        nc.scalar.dma_start(out=cen_b[:], in_=center.rearrange("a b (n c) -> (a b n) c", c=3))
        ks_b = keep.tile([P, 1], BF16, name="ks_b")
        nc.scalar.dma_start(out=ks_b[:], in_=keep_score.rearrange("a b (n o) -> (a b n) o", o=1))
        bgb_b = keep.tile([P, 1], BF16, name="bgb_b")
        nc.scalar.dma_start(out=bgb_b[:], in_=background_bias.partition_broadcast(P))

        for which in ("q", "g"):
            for h in range(2):
                for quad in range(4):
                    dst = planes[which][32 * quad : 32 * quad + 16, h, :]
                    src = scales_in[which][4 * h : 4 * h + 4, 4 * quad : 4 * quad + 4, :]
                    nc.gpsimd.dma_start(out=dst.bitcast(F32), in_=src.bitcast(F32))

        def spread(row, n, bank, name):
            t = psum.tile([P, n], F32, name=name, tag="bk%d" % bank)
            nc.tensor.matmul(
                out=t[:], lhsT=ident_b[:, row : row + 1].to_broadcast([P, P]), rhs=rows[:, 0:n], start=True, stop=True
            )
            return t

        bias_bc = {}

        def spread_bias(which, row0):
            bias_bc[which] = keep.tile([P, D_OUT], BF16, name="bias_bc_" + which)
            for b in range(4):
                t = spread(row0 + b, BANK, 4 + b, "bias_ps")
                dst = bias_bc[which][:, BANK * b : BANK * (b + 1)]
                if b % 2 == 0:
                    nc.scalar.copy(out=dst, in_=t[:])
                else:
                    nc.vector.tensor_copy(out=dst, in_=t[:])

        x_words = {}

        def prep_x(which, x_sb, first_bank):
            xv = x_sb[:].bitcast(F32)
            grouped = keep.tile([P, PASSES, P, 4], BF16, name="grouped", tag="grouped", align_bytes=64)
            xw = keep.tile([P, PASSES * P], U32, name="xw_" + which, align_bytes=64)
            xs = keep.tile([P, PASSES * P], U8, name="xs_" + which, align_bytes=64)

            def move(pair):
                xt = psum.tile([P, 2, 2, P], F32, name="xt", tag="bk%d" % (first_bank + pair))
                for g2 in range(2):
                    g = 2 * pair + g2
                    for u in range(2):
                        nc.tensor.transpose(xt[:, g2, u, :], xv[:, 256 * g + u : 256 * (g + 1) : 2], ident_f[:])
                dst = (
                    grouped[:, 2 * pair : 2 * pair + 2]
                    .rearrange("p g r t -> p g (r t)")
                    .bitcast(F32)
                    .rearrange("p g (r u) -> p g r u", u=2)
                )
                src = xt[:].rearrange("p g u r -> p g r u")
                if pair % 2 == 0:
                    nc.scalar.copy(out=dst, in_=src)
                else:
                    nc.vector.tensor_copy(out=dst, in_=src)

            def quantise(pair):
                nc.vector.quantize_mx(
                    out=xw[:, 256 * pair : 256 * (pair + 1)].bitcast(FP8X4),
                    scales=xs[:, 256 * pair : 256 * (pair + 1)],
                    in_=grouped[:, 2 * pair : 2 * pair + 2].rearrange("p g r t -> p (g r t)"),
                )

            move(0)
            move(1)
            quantise(0)
            move(2)
            move(3)
            quantise(1)
            quantise(2)
            quantise(3)
            x_words[which] = (xw, xs)

        col_tiles = {
            "q": [(0, 512, 0), (512, 1024, 1), (1024, 1536, 2), (1536, 2048, 3)],
            "g": [(0, 512, 4), (512, 1024, 5), (1024, 1536, 6), (1536, 1792, 7), (1792, 2048, 0)],
        }
        acc = {}
        y = {}
        ssp = {}

        def open_acc(which):
            acc[which] = [
                psum.tile([P, n1 - n0], F32, name="acc_%s%d" % (which, i), tag="bk%d" % bank)
                for i, (n0, n1, bank) in enumerate(col_tiles[which])
            ]
            y[which] = keep.tile([P, D_OUT], F32, name="y", tag="y")
            ssp[which] = keep.tile([P, len(acc[which])], F32, name="ssp_" + which)

        def passes(which, g, w0, w1):
            xw, xs = x_words[which]
            h = g // 4
            k = 4 * (g % 4)
            w = w_tiles[(which, g, w0)]
            for i, (n0, n1, bank) in enumerate(col_tiles[which]):
                if n0 < w0 or n1 > w1:
                    continue
                nc.tensor.matmul_mx(
                    out=acc[which][i][:],
                    lhsT=xw[:, P * g : P * (g + 1)].bitcast(FP8X4),
                    lhsT_scale=xs[:, P * g : P * (g + 1)],
                    rhs=w[:, n0 - w0 : n1 - w0].bitcast(FP8X4),
                    rhs_scale=planes[which][k:P, h, n0:n1],
                    start=(g == 0),
                    stop=(g == PASSES - 1),
                )

        def bias_and_squares(which, i):
            n0, n1, bank = col_tiles[which][i]
            nc.vector.tensor_tensor(
                out=y[which][:, n0:n1], in0=acc[which][i][:], in1=bias_bc[which][:, n0:n1], op=ALU.add
            )
            junk = work.tile([P, BANK], F32, name="junk")
            nc.scalar.activation(
                out=junk[:, 0 : n1 - n0], in_=y[which][:, n0:n1], func=ACT.Square, accum_out=ssp[which][:, i : i + 1]
            )

        f_words = {}

        def inverse_norm(which):
            last = len(acc[which]) - 1
            early = keep.tile([P, 1], F32, name="early_" + which)
            nc.vector.tensor_reduce(out=early[:], in_=ssp[which][:, 0:last], axis=AX.X, op=ALU.add)
            raw = keep.tile([P, 1], F32, name="raw_" + which)
            nc.scalar.activation(
                out=raw[:],
                in_=ssp[which][:, last : last + 1],
                func=ACT.Abs_reciprocal_sqrt,
                bias=early[:, 0:1],
                scale=1.0,
            )
            rn = keep.tile([P, 1], F32, name="rn_" + which)
            nc.vector.tensor_scalar(out=rn[:], in0=raw[:], scalar1=1e12, scalar2=None, op0=ALU.min)
            return rn

        def pack(which, rn, banks):
            fw = keep.tile([P, 4 * P], U32, name="fw_" + which, align_bytes=64)
            fs = keep.tile([P, 4 * P], U8, name="fs_" + which, align_bytes=64)
            grp = keep.tile([P, 4, P, 4], BF16, name="grp", tag="grp", align_bytes=64)
            yn = keep.tile([P, D_OUT], BF16, name="yn", tag="yn")
            for c in range(4):
                cols = slice(BANK * c, BANK * (c + 1))
                nc.vector.tensor_scalar(
                    out=yn[:, cols], in0=y[which][:, cols], scalar1=rn[:, 0:1], scalar2=None, op0=ALU.mult
                )
            yw = yn[:].bitcast(F32)
            for c in range(4):
                pt = psum.tile([P, 2, P], F32, name="pt_" + which, tag="bk%d" % banks[c])
                for u in range(2):
                    nc.tensor.transpose(pt[:, u, :], yw[:, 256 * c + P * u : 256 * c + P * (u + 1)], ident_f[:])
                dst = grp[:, c].rearrange("p r t -> p (r t)").bitcast(F32).rearrange("p (r u) -> p r u", u=2)
                src = pt[:].rearrange("p u r -> p r u")
                if c < 2:
                    nc.vector.tensor_copy(out=dst, in_=src)
                else:
                    nc.scalar.copy(out=dst, in_=src)
            for c in range(4):
                nc.vector.quantize_mx(
                    out=fw[:, P * c : P * (c + 1)].bitcast(FP8X4),
                    scales=fs[:, P * c : P * (c + 1)],
                    in_=grp[:, c].rearrange("p r t -> p (r t)"),
                )
            f_words[which] = (fw, fs)

        spread_bias("q", ROW_BQ)
        prep_x("q", x_q, 0)

        boxes = keep.tile([P, 2, 448], F32, name="boxes")
        for j in range(2):
            t = spread(ROW_BOX + j, 448, 4 + j, "box_ps")
            nc.scalar.copy(out=boxes[:, j, :], in_=t[:])
        box_v = boxes[:].rearrange("p j (m c) -> p (j m) c", c=7)
        pres_bc = keep.tile([P, P], F32, name="pres_bc")
        t = spread(ROW_PRES, P, 6, "pres_ps")
        nc.scalar.copy(out=pres_bc[:], in_=t[:])

        open_acc("q")
        passes("q", 0, 0, D_OUT)
        spread_bias("g", ROW_BG)

        kc = keep.tile([P, 1], F32, name="kc")
        nc.vector.tensor_scalar(out=kc[:], in0=ks_b[:], scalar1=1e-4, scalar2=1.0 - 1e-4, op0=ALU.max, op1=ALU.min)
        ln_k = keep.tile([P, 1], F32, name="ln_k")
        nc.scalar.activation(out=ln_k[:], in_=kc[:], func=ACT.Ln)
        ln_1k = keep.tile([P, 1], F32, name="ln_1k")
        nc.scalar.activation(out=ln_1k[:], in_=kc[:], func=ACT.Ln, bias=1.0, scale=-1.0)

        cen = keep.tile([P, 3], F32, name="cen")
        nc.vector.tensor_copy(out=cen[:], in_=cen_b[:])
        size_v = box_v[:, :, 3:6].rearrange("p m c -> p c m")
        ext = keep.tile([P, 3, P], F32, name="ext")
        nc.vector.scalar_tensor_tensor(out=ext[:], in0=size_v, scalar=-1.0, in1=size_v, op0=ALU.mult, op1=ALU.max)
        nc.vector.tensor_scalar(out=ext[:], in0=ext[:], scalar1=0.5, scalar2=0.75, op0=ALU.max, op1=ALU.mult)
        inv = keep.tile([P, 3, P], F32, name="inv")
        nc.vector.reciprocal(out=inv[:], in_=ext[:])
        dist = keep.tile([P, 3, P], F32, name="dist")
        for c in range(3):
            nc.vector.scalar_tensor_tensor(
                out=dist[:, c, :],
                in0=box_v[:, :, c],
                scalar=cen[:, c : c + 1],
                in1=inv[:, c, :],
                op0=ALU.subtract,
                op1=ALU.mult,
            )
        adist = keep.tile([P, 3, P], F32, name="adist")
        nc.vector.scalar_tensor_tensor(out=adist[:], in0=dist[:], scalar=-1.0, in1=dist[:], op0=ALU.mult, op1=ALU.max)
        far = keep.tile([P, P], F32, name="far")
        nc.vector.tensor_reduce(out=far[:], in_=adist[:].rearrange("p c m -> p m c"), axis=AX.X, op=ALU.max)
        gate = keep.tile([P, P], F32, name="gate")
        nc.vector.tensor_scalar(out=gate[:], in0=far[:], scalar1=-3.0, scalar2=3.0, op0=ALU.mult, op1=ALU.add)
        nc.vector.tensor_scalar(out=gate[:], in0=gate[:], scalar1=-8.0, scalar2=8.0, op0=ALU.max, op1=ALU.min)
        half_keep = keep.tile([P, 1], F32, name="half_keep")
        nc.vector.tensor_scalar(
            out=half_keep[:], in0=ln_k[:], scalar1=ln_1k[:, 0:1], scalar2=0.5, op0=ALU.subtract, op1=ALU.mult
        )
        base = keep.tile([P, P + 1], F32, name="base")
        nc.vector.tensor_copy(out=base[:, 0:1], in_=bgb_b[:])
        nc.vector.scalar_tensor_tensor(
            out=base[:, 1 : P + 1], in0=gate[:], scalar=half_keep[:, 0:1], in1=pres_bc[:], op0=ALU.add, op1=ALU.add
        )
        neg_max = keep.tile([P, 1], F32, name="neg_max")
        nc.vector.tensor_reduce(out=neg_max[:], in_=base[:], axis=AX.X, op=ALU.max, negate=True)
        e_base = keep.tile([P, P + 1], F32, name="e_base")
        nc.scalar.activation(out=e_base[:], in_=base[:], func=ACT.Exp, bias=neg_max[:, 0:1], scale=1.0)

        for g in range(1, 4):
            passes("q", g, 0, D_OUT)
        prep_x("g", x_g, 4)
        for g in range(4, PASSES):
            passes("q", g, 0, D_OUT)
        for i in range(4):
            bias_and_squares("q", i)
        rn_q = inverse_norm("q")

        open_acc("g")
        passes("g", 0, 0, D_OUT)
        passes("g", 1, 0, D_OUT)
        pack("q", rn_q, [1, 2, 3, 1])
        for g in range(2, 6):
            passes("g", g, 0, D_OUT)
        done = 0
        for pieces in last_pieces:
            for g, n0, n1 in pieces:
                passes("g", g, n0, n1)
            while col_tiles["g"][done][1] < n1:
                bias_and_squares("g", done)
                done += 1
            bias_and_squares("g", done)
            done += 1
        rn_g = inverse_norm("g")
        table = keep.tile([P, 1], F32, name="table")
        nc.scalar.activation(out=table[:], in_=neg_half[:], func=ACT.Exp)
        warm = psum.tile([P, BANK], F32, name="warm", tag="bk4")
        for i in range(WARM):
            nc.tensor.matmul(out=warm[:], lhsT=ident_b[:], rhs=bias_bc["g"][:, 0:BANK], start=True, stop=True)
        pack("g", rn_g, [1, 2, 3, 5])

        sim = psum.tile([P, P], F32, name="sim", tag="bk4")
        gw, gs = f_words["g"]
        qw, qs = f_words["q"]
        for c in range(4):
            nc.tensor.matmul_mx(
                out=sim[:],
                lhsT=gw[:, P * c : P * (c + 1)].bitcast(FP8X4),
                lhsT_scale=gs[:, P * c : P * (c + 1)],
                rhs=qw[:, P * c : P * (c + 1)].bitcast(FP8X4),
                rhs_scale=qs[:, P * c : P * (c + 1)],
                start=(c == 0),
                stop=(c == 3),
            )
        nc.scalar.activation(out=e_sim[:, 1 : P + 1], in_=sim[:], func=ACT.Exp, scale=6.0)
        prod = keep.tile([P, P + 1], F32, name="prod")
        total = keep.tile([P, 1], F32, name="total")
        nc.vector.scalar_tensor_tensor(
            out=prod[:], in0=e_sim[:], scalar=1.0, in1=e_base[:], op0=ALU.mult, op1=ALU.mult, accum_out=total[:]
        )
        inv_total = keep.tile([P, 1], F32, name="inv_total")
        nc.vector.reciprocal(out=inv_total[:], in_=total[:])
        probs = keep.tile([P, P + 1], F32, name="probs")
        nc.vector.tensor_scalar(out=probs[:], in0=prod[:], scalar1=inv_total[:, 0:1], scalar2=None, op0=ALU.mult)
        nc.sync.dma_start(out=out.rearrange("a n j -> (a n) j"), in_=probs[:])
